import numpy as np
import ml_dtypes


def mxq(x, axis, fmt="e4m3"):
    dtype, down = {"e4m3": (ml_dtypes.float8_e4m3fn, 7), "e5m2": (ml_dtypes.float8_e5m2, 14)}[fmt]
    v = np.moveaxis(np.asarray(x, np.float32).astype(ml_dtypes.bfloat16).astype(np.float64), axis, -1)
    blocks = v.reshape(v.shape[:-1] + (-1, 32))
    amax = np.abs(blocks).max(-1, keepdims=True)
    byte = np.maximum(np.where(amax > 0, np.frexp(amax)[1] - 1 + 127, 0) - down, 1)
    scale = np.exp2(byte - 127.0)
    codes = (blocks / scale).astype(np.float32).astype(dtype).astype(np.float64)
    return np.moveaxis((codes * scale).reshape(v.shape), -1, axis)


WIDE = False


def mx_kscale(k):
    if not WIDE:
        return np.ones(k)
    levels = np.array([10, -10, 5, -5, 0])
    if k % 512:
        return np.exp2(np.random.permutation(np.resize(levels, k // 32))).repeat(32)
    a = np.empty((k // 512, 16))
    for p in range(k // 512):
        a[p, :8] = np.random.permutation(np.resize(levels, 8))
        for g in range(8):
            far = levels[np.abs(levels - a[p, g]) >= 10]
            a[p, g + 8] = far[np.random.randint(len(far))]
    return np.exp2(a.ravel()).repeat(32)


BF16 = ml_dtypes.bfloat16


def bf(x):
    return np.asarray(x, np.float32).astype(BF16)


def f64(x):
    return np.asarray(x).astype(np.float64)


E2M1 = np.array([0.0, 0.5, 1.0, 1.5, 2.0, 3.0, 4.0, 6.0, -0.0, -0.5, -1.0, -1.5, -2.0, -3.0, -4.0, -6.0])


def pack_weight(w, fmt):
    k, n = w.shape
    w = f64(bf(w)).reshape(k // 32, 32, n)
    amax = np.abs(w).max(1)
    if fmt == "e4m3":
        byte = np.frexp(amax)[1] - 1 + 127 - 7
    else:
        mant, ex = np.frexp(amax / 6.0)
        byte = np.where(mant > 0.5, ex, ex - 1) + 127
    byte = np.clip(np.where(amax > 0, byte, 1), 1, 254)
    scaled = (w * np.exp2(127.0 - byte)[:, None, :]).reshape(k, n).astype(np.float32)
    by_word = np.ascontiguousarray(scaled.reshape(k // 512, 128, 4, n).transpose(0, 1, 3, 2))
    if fmt == "e4m3":
        words = by_word.astype(ml_dtypes.float8_e4m3fn).view(np.uint8)
    else:
        c = by_word.astype(ml_dtypes.float4_e2m1fn).view(np.uint8) & 0xF
        words = c[..., 0::2] | (c[..., 1::2] << 4)
    return np.ascontiguousarray(words), np.ascontiguousarray(byte.astype(np.uint8).reshape(k // 512, 16, n))


def unpack_weight(words, scales, fmt):
    g, p, n, _ = words.shape
    if fmt == "e4m3":
        vals = np.ascontiguousarray(words).view(ml_dtypes.float8_e4m3fn).astype(np.float64)
    else:
        nib = np.empty((g, p, n, 4), np.uint8)
        nib[..., 0::2] = words & 0xF
        nib[..., 1::2] = words >> 4
        vals = E2M1[nib]
    vals = vals * np.repeat(np.exp2(scales.astype(np.float64) - 127.0), 8, axis=1)[..., None]
    return vals.transpose(0, 1, 3, 2).reshape(g * 512, n)


B, S, D, H, DH, F = 4, 1024, 1024, 4, 128, 512
E = H * DH
EPS = 1e-5
NTERMS = 120


def layernorm(x, g, b):
    mu = x.mean(-1, keepdims=True)
    var = np.square(x - mu).mean(-1, keepdims=True)
    return (x - mu) / np.sqrt(var + EPS) * g + b


def erf(v):
    a = np.minimum(np.maximum(v, -6.0), 6.0)
    term = a.copy()
    total = a.copy()
    for n in range(1, NTERMS):
        term = term * (2.0 * a * a) / (2.0 * n + 1.0)
        total = total + term
    return 2.0 / np.sqrt(np.pi) * np.exp(-a * a) * total


def gelu_erf(v):
    return 0.5 * v * (1.0 + erf(v / np.sqrt(2.0)))


def draw0():
    s, t = mx_kscale(E), mx_kscale(D)
    x = np.random.standard_normal((B, S, D)) + 0.5 * np.random.standard_normal((B, S, 1))
    h_attn = bf(0.2 * np.random.standard_normal((B, S, E)) * s)
    w_out_words, w_out_scales = pack_weight((np.random.standard_normal((D, E)) * 2.0 / np.sqrt(E) / s).T, "e4m3")
    w_fc1_words, w_fc1_scales = pack_weight((np.random.standard_normal((F, D)) / np.sqrt(D) / t).T, "e4m3")
    return {"h_attn": h_attn,
            "x": bf(x),
            "w_out_words": w_out_words,
            "w_out_scales": w_out_scales,
            "w_fc1_words": w_fc1_words,
            "w_fc1_scales": w_fc1_scales,
            "g2": bf((1.0 + 0.1 * np.random.standard_normal(D)) * t),
            "b2": bf(0.1 * np.random.standard_normal(D) * t)}


def core(h_attn, x, w_out_words, w_out_scales, w_fc1_words, w_fc1_scales, g2, b2):
    x_mid = f64(x) + (mxq(f64(h_attn), 2, "e4m3") @ unpack_weight(w_out_words, w_out_scales, "e4m3"))
    h = layernorm(x_mid, f64(g2), f64(b2))
    u = mxq(h, 2, "e4m3") @ unpack_weight(w_fc1_words, w_fc1_scales, "e4m3")
    return x_mid, gelu_erf(u)


def e4m3fn_bytes(y):
    return np.clip(np.asarray(y, np.float64), -448.0, 448.0).astype(np.float32).astype(ml_dtypes.float8_e4m3fn).view(np.uint8)


def e4m3fn_values(b):
    return np.asarray(b, np.uint8).view(ml_dtypes.float8_e4m3fn).astype(np.float64)


def setup_inputs():
    d = draw0()
    x0 = np.asarray(d['h_attn']).astype(np.float64)
    s = (np.max(np.abs(x0), axis=(0, 1), keepdims=True) / 448.0).astype(np.float32)
    out = {}
    for k, v in d.items():
        if k == 'h_attn':
            out['h_attn_bytes'] = e4m3fn_bytes(x0 / s.astype(np.float64))
            out['h_attn_scale'] = s
        else:
            out[k] = v
    return out


def reference(h_attn_bytes, h_attn_scale, x, w_out_words, w_out_scales, w_fc1_words, w_fc1_scales, g2, b2):
    return core(e4m3fn_values(h_attn_bytes) * h_attn_scale.astype(np.float64), x, w_out_words, w_out_scales, w_fc1_words, w_fc1_scales, g2, b2)

@@ -1,0 +1,326 @@
+from contextlib import ExitStack
+
+import concourse.mybir as mybir
+from concourse.masks import make_identity
+
+F32 = mybir.dt.float32
+BF16 = mybir.dt.bfloat16
+I32 = mybir.dt.int32
+U32 = mybir.dt.uint32
+U8 = mybir.dt.uint8
+FP8 = mybir.dt.float8_e4m3fn
+FP8X4 = mybir.dt.float8_e4m3fn_x4
+ALU = mybir.AluOpType
+ACT = mybir.ActivationFunctionType
+
+P = 128
+TOKENS, E, D, F = 4096, 512, 1024, 512
+TILES = TOKENS // P
+MT = 4
+MACROS = TILES // MT
+WIDTHS = [1, 1, 2] + 6 * [4] + [2, 2]
+GROUPS = [(sum(WIDTHS[:k]), w) for k, w in enumerate(WIDTHS)]
+GROUP_OF = [k for k, w in enumerate(WIDTHS) for i in range(w)]
+EPS = 1e-5
+FLOPS = 2 * TOKENS * E * D + 2 * TOKENS * D * F
+V_EVAC = ()
+Z_ENGINE = "gpsimd"
+
+
+def tile_minitransformerlayer_pb_t_w8_kernel(
+    tc, h_attn_bytes, h_attn_scale, x, w_out_words, w_out_scales, w_fc1_words, w_fc1_scales, g2, b2, out_0, out_1
+):
+    nc = tc.nc
+    bytes_v = h_attn_bytes.flatten_outer_dims().rearrange("(m p i) k -> m p i k", p=P, i=MT)
+    x_v = x.flatten_outer_dims().rearrange("(m p i) d -> m p i d", p=P, i=MT)
+    mid_v = out_0.flatten_outer_dims().rearrange("(m p i) d -> m p i d", p=P, i=MT)
+    act_v = out_1.flatten_outer_dims().rearrange("(m p i) f -> m p i f", p=P, i=MT)
+
+    with ExitStack() as ctx:
+        keep = ctx.enter_context(tc.tile_pool(name="keep", bufs=1))
+        pool = ctx.enter_context(tc.tile_pool(name="pool", bufs=2))
+        psum = ctx.enter_context(tc.psum_pool(name="psum", bufs=2))
+        ctx.enter_context(tc.manual_schedule())
+
+        ident = keep.tile([P, P], F32, name="ident")
+        scale_bc = keep.tile([P, E], F32, name="scale_bc", align_bytes=64)
+        w1_words = keep.tile([P, D], I32, name="w1_words", align_bytes=64)
+        w1_scales = keep.tile([P, D], U8, name="w1_scales", align_bytes=64)
+        w2_words = keep.tile([P, 2, F], I32, name="w2_words", align_bytes=64)
+        w2_scales = keep.tile([P, 2, F], U8, name="w2_scales", align_bytes=64)
+        gb_raw = keep.tile([P, 2, 8], BF16, name="gb_raw")
+        b_raw = keep.tile([P, 2, 8], BF16, name="b_raw")
+        g_col = keep.tile([P, 8], F32, name="g_col")
+        b_col = keep.tile([P, 8], F32, name="b_col")
+        neg_half = keep.tile([P, 1], F32, name="neg_half")
+        warm = keep.tile([P, 1], F32, name="warm")
+        sq_dump = keep.tile([P, D], BF16, name="sq_dump")
+
+        a_bytes, x_t, a_bf, a_codes, a_scales = {}, {}, {}, {}, {}
+        groups, mid, sums, negmu, ssq, rstd, z_t = {}, {}, {}, {}, {}, {}, {}
+        mm1_ps, planes, hgs, h_codes, h_scales, mm2_ps, act_t, zps, aps = {}, {}, {}, {}, {}, {}, {}, {}, {}
+
+        def load_a(m):
+            a_bytes[m] = pool.tile([P, MT, E], U8, name="a_bytes", bufs=4, align_bytes=64)
+            nc.sync.dma_start(out=a_bytes[m][:], in_=bytes_v[m])
+
+        def load_x(m):
+            x_t[m] = pool.tile([P, MT, D], BF16, name="x_t", bufs=3, align_bytes=64)
+            for h in range(2):
+                nc.sync.dma_start(out=x_t[m][:, 2 * h : 2 * h + 2, :], in_=x_v[m][:, 2 * h : 2 * h + 2, :])
+
+        def dequant(t):
+            m, i = divmod(t, MT)
+            a_bf[t] = pool.tile([P, E], BF16, name="a_bf", bufs=5, align_bytes=64)
+            nc.vector.tensor_tensor(
+                out=a_bf[t][:], in0=a_bytes[m][:, i, :].bitcast(FP8), in1=scale_bc[:], op=ALU.mult
+            )
+
+        def a_transpose(q):
+            aps[q] = psum.tile([P, 4, P], F32, name="a_ps", bufs=1)
+            for i in range(2):
+                words = a_bf[2 * q + i][:].bitcast(F32)
+                for u in range(2):
+                    nc.tensor.transpose(aps[q][:, 2 * i + u, :], words[:, u : E // 2 : 2], ident[:])
+
+        def a_evac(q):
+            groups[q] = pool.tile([P, 8 * P], BF16, name="a_group", bufs=2, align_bytes=64)
+            nc.scalar.copy(
+                out=groups[q][:].bitcast(F32).rearrange("p (i n u) -> p i n u", i=2, u=2),
+                in_=aps[q][:].rearrange("p (i u) n -> p i n u", u=2),
+            )
+
+        def a_quant(q):
+            a_codes[q] = pool.tile([P, 2 * P], U32, name="a_codes", bufs=3, align_bytes=64)
+            a_scales[q] = pool.tile([P, 2 * P], U8, name="a_scales", bufs=3, align_bytes=64)
+            nc.vector.quantize_mx(out=a_codes[q][:].bitcast(FP8X4), scales=a_scales[q][:], in_=groups[q][:])
+
+        def mm1(t):
+            q, i = divmod(t, 2)
+            cols = slice(i * P, (i + 1) * P)
+            for c in range(2):
+                n = slice(c * 512, (c + 1) * 512)
+                mm1_ps[t, c] = psum.tile([P, 512], F32, name="mm1_ps", bufs=3)
+                nc.tensor.matmul_mx(
+                    out=mm1_ps[t, c][:],
+                    lhsT=a_codes[q][:, cols].bitcast(FP8X4),
+                    lhsT_scale=a_scales[q][:, cols],
+                    rhs=w1_words[:, n].bitcast(FP8X4),
+                    rhs_scale=w1_scales[:, n],
+                    start=True,
+                    stop=True,
+                )
+
+        def resid(t):
+            m, i = divmod(t, MT)
+            q, r = divmod(t, 2)
+            if r == 0:
+                mid[q] = pool.tile([P, 2, D], F32, name="mid", bufs=4, align_bytes=64)
+            sums[t] = pool.tile([P, 2], F32, name="sums", bufs=4)
+            for c in range(2):
+                n = slice(c * 512, (c + 1) * 512)
+                nc.vector.scalar_tensor_tensor(
+                    out=mid[q][:, r, n],
+                    in0=mm1_ps[t, c][:],
+                    scalar=1.0,
+                    in1=x_t[m][:, i, n],
+                    op0=ALU.mult,
+                    op1=ALU.add,
+                    accum_out=sums[t][:, c : c + 1],
+                )
+
+        def mean(t):
+            negmu[t] = pool.tile([P, 1], F32, name="negmu", bufs=4)
+            nc.gpsimd.tensor_scalar(
+                out=negmu[t][:],
+                in0=sums[t][:, 0:1],
+                scalar1=sums[t][:, 1:2],
+                scalar2=-1.0 / D,
+                op0=ALU.add,
+                op1=ALU.mult,
+            )
+
+        def square(t):
+            q, r = divmod(t, 2)
+            ssq[t] = pool.tile([P, 1], F32, name="ssq", bufs=4)
+            nc.scalar.activation(
+                out=sq_dump[:], in_=mid[q][:, r, :], func=ACT.Square, bias=negmu[t][:], accum_out=ssq[t][:]
+            )
+
+        def norm(t):
+            q, r = divmod(t, 2)
+            var = pool.tile([P, 1], F32, name="var", bufs=2)
+            rstd[t] = pool.tile([P, 1], F32, name="rstd", bufs=2)
+            nc.gpsimd.tensor_scalar(
+                out=var[:], in0=ssq[t][:], scalar1=1.0 / D, scalar2=EPS, op0=ALU.mult, op1=ALU.add
+            )
+            nc.gpsimd.tensor_tensor(out=rstd[t][:], in0=var[:], in1=neg_half[:], op=ALU.pow)
+            z_t[t] = pool.tile([P, D], F32, name="z_t", bufs=12, align_bytes=64)
+            eng = nc.gpsimd if Z_ENGINE == "gpsimd" else nc.vector
+            eng.tensor_scalar(
+                out=z_t[t][:].rearrange("q (g t p) -> q g t p", g=2, t=4),
+                in0=mid[q][:, r, :].rearrange("q (g p t) -> q g t p", g=2, t=4),
+                scalar1=negmu[t][:],
+                scalar2=rstd[t][:],
+                op0=ALU.add,
+                op1=ALU.mult,
+            )
+
+        def store_mid(q):
+            m, h = divmod(q, 2)
+            nc.sync.dma_start(out=mid_v[m][:, 2 * h : 2 * h + 2, :], in_=mid[q][:])
+
+        def z_transpose(m, j):
+            first, w = GROUPS[m]
+            zps[m, j] = psum.tile([P, w * P], F32, name="z_ps", bufs=2)
+            for i in range(w):
+                nc.tensor.transpose(
+                    zps[m, j][:, i * P : (i + 1) * P], z_t[first + i][:, j * P : (j + 1) * P], ident[:]
+                )
+
+        def affine(m, j, on_vector):
+            g, t = divmod(j, 4)
+            if t == 0:
+                planes[m, g] = pool.tile([P, 4, GROUPS[m][1] * P], BF16, name="planes", bufs=5, align_bytes=64)
+            if on_vector:
+                nc.vector.tensor_scalar(
+                    out=planes[m, g][:, t, :],
+                    in0=zps[m, j][:],
+                    scalar1=g_col[:, j : j + 1],
+                    scalar2=b_col[:, j : j + 1],
+                    op0=ALU.mult,
+                    op1=ALU.add,
+                )
+            else:
+                nc.scalar.activation(
+                    out=planes[m, g][:, t, :],
+                    in_=zps[m, j][:],
+                    func=ACT.Identity,
+                    scale=g_col[:, j : j + 1],
+                    bias=b_col[:, j : j + 1],
+                )
+
+        def interleave(m, g):
+            hgs[m, g] = pool.tile([P, GROUPS[m][1] * P, 4], BF16, name="h_group", bufs=4, align_bytes=64)
+            nc.vector.tensor_copy(out=hgs[m, g][:], in_=planes[m, g][:].rearrange("p t n -> p n t"))
+
+        def h_quant(m, g):
+            h_codes[m, g] = pool.tile([P, GROUPS[m][1] * P], U32, name="h_codes", bufs=6, align_bytes=64)
+            h_scales[m, g] = pool.tile([P, GROUPS[m][1] * P], U8, name="h_scales", bufs=6, align_bytes=64)
+            nc.vector.quantize_mx(
+                out=h_codes[m, g][:].bitcast(FP8X4),
+                scales=h_scales[m, g][:],
+                in_=hgs[m, g][:].rearrange("p n t -> p (n t)"),
+            )
+
+        def mm2(t):
+            m = GROUP_OF[t]
+            i = t - GROUPS[m][0]
+            cols = slice(i * P, (i + 1) * P)
+            mm2_ps[t] = psum.tile([P, F], F32, name="mm2_ps", bufs=2)
+            for g in range(2):
+                nc.tensor.matmul_mx(
+                    out=mm2_ps[t][:],
+                    lhsT=h_codes[m, g][:, cols].bitcast(FP8X4),
+                    lhsT_scale=h_scales[m, g][:, cols],
+                    rhs=w2_words[:, g, :].bitcast(FP8X4),
+                    rhs_scale=w2_scales[:, g, :],
+                    start=(g == 0),
+                    stop=(g == 1),
+                )
+
+        def gelu(t):
+            q, r = divmod(t, 2)
+            if r == 0:
+                act_t[q] = pool.tile([P, 2, F], F32, name="act_t", bufs=6, align_bytes=64)
+            nc.scalar.activation(out=act_t[q][:, r, :], in_=mm2_ps[t][:], func=ACT.Gelu)
+
+        def store_act(q):
+            m, h = divmod(q, 2)
+            nc.sync.dma_start(out=act_v[m][:, 2 * h : 2 * h + 2, :], in_=act_t[q][:])
+
+        nc.vector.memset(w1_scales[:].bitcast(I32), 0)
+        nc.vector.memset(w2_scales[:].rearrange("p g n -> p (g n)").bitcast(I32), 0)
+        nc.vector.memset(neg_half[:], -0.5)
+        nc.vector.memset(warm[:], 0.0)
+        make_identity(nc, ident[:])
+        nc.scalar.activation(out=warm[:], in_=warm[:], func=ACT.Gelu)
+
+        nc.sync.dma_start(out=scale_bc[:], in_=h_attn_scale.rearrange("a b k -> (a b k)").partition_broadcast(P))
+        load_a(0)
+        nc.sync.dma_start(out=w1_words[:], in_=w_out_words[0].rearrange("p n t -> p (n t)").bitcast(I32))
+        s1 = w_out_scales[0].bitcast(I32)
+        for quad in range(4):
+            nc.sync.dma_start(
+                out=w1_scales[32 * quad : 32 * quad + 4, :].bitcast(I32), in_=s1[4 * quad : 4 * quad + 4, :]
+            )
+        load_a(1)
+        load_x(0)
+        nc.sync.dma_start(out=gb_raw[:, :, 0:4], in_=g2.rearrange("(g p t) -> p g t", p=P, t=4))
+        nc.sync.dma_start(out=b_raw[:, :, 0:4], in_=b2.rearrange("(g p t) -> p g t", p=P, t=4))
+        load_a(2)
+        load_x(1)
+        nc.sync.dma_start(
+            out=w2_words[:],
+            in_=w_fc1_words.rearrange("g p n t -> p g (n t)").bitcast(I32),
+        )
+        s2 = w_fc1_scales.bitcast(I32).rearrange("g q n -> q g n")
+        for quad in range(4):
+            nc.sync.dma_start(
+                out=w2_scales[32 * quad : 32 * quad + 4, :, :].bitcast(I32), in_=s2[4 * quad : 4 * quad + 4]
+            )
+        nc.gpsimd.tensor_copy(out=g_col[:].rearrange("p (g t) -> p g t", g=2), in_=gb_raw[:, :, 0:4])
+        nc.gpsimd.tensor_copy(out=b_col[:].rearrange("p (g t) -> p g t", g=2), in_=b_raw[:, :, 0:4])
+
+        BANKS, IL, HQ, MM2 = {}, {}, {}, {}
+        for k, (first, w) in enumerate(GROUPS):
+            s0 = first + w + 2
+            for j in range(8):
+                BANKS.setdefault(s0 + j * w // 8, []).append((k, j))
+            ends = ((w + 1) // 2, w)
+            for g in range(2):
+                IL.setdefault(s0 + ends[g] + 1, []).append((k, g))
+                HQ.setdefault(s0 + ends[g] + 2, []).append((k, g))
+            for i in range(w):
+                MM2.setdefault(s0 + w + 3 + i, []).append(first + i)
+        for s in range(-6, TILES + 20):
+            if 0 <= s < TILES and s % MT == 0 and s // MT + 3 < MACROS:
+                load_a(s // MT + 3)
+            if 0 <= s < TILES and s % MT == 0 and s // MT + 2 < MACROS:
+                load_x(s // MT + 2)
+            if 0 <= s - 2 < TILES:
+                norm(s - 2)
+            q, r = divmod(s + 4, 2)
+            if r == 0 and 0 <= q < TILES // 2:
+                a_transpose(q)
+            if 0 <= s + 1 < TILES:
+                mm1(s + 1)
+            for t in MM2.get(s, []):
+                mm2(t)
+            if 0 <= s < TILES:
+                resid(s)
+                mean(s)
+            for m, g in HQ.get(s, []):
+                h_quant(m, g)
+            for m, g in IL.get(s, []):
+                interleave(m, g)
+            q, r = divmod(s + 3, 2)
+            if r == 0 and 0 <= q < TILES // 2:
+                a_evac(q)
+            for m, j in BANKS.get(s - 1, []):
+                affine(m, j, j in V_EVAC or (GROUPS[m][0] >= 28 and j % 2 == 1))
+            for m, j in BANKS.get(s, []):
+                z_transpose(m, j)
+            if 0 <= s - 1 < TILES:
+                square(s - 1)
+            for t in MM2.get(s - 1, []):
+                gelu(t)
+            if 0 <= s + 6 < TILES:
+                dequant(s + 6)
+            if r == 0 and 0 <= q < TILES // 2:
+                a_quant(q)
+            if s % 2 == 1 and 0 <= s < TILES:
+                store_mid(s // 2)
+            for t in MM2.get(s - 1, []):
+                if t % 2 == 1:
+                    store_act(t // 2)

@@ -24,7 +24,6 @@ GROUP_OF = [k for k, w in enumerate(WIDTHS) for i in range(w)]
 EPS = 1e-5
 FLOPS = 2 * TOKENS * E * D + 2 * TOKENS * D * F
 V_EVAC = ()
-Z_ENGINE = "gpsimd"
 
 
 def tile_minitransformerlayer_pb_t_w8_kernel(
@@ -150,21 +149,25 @@ def tile_minitransformerlayer_pb_t_w8_kernel(
         def norm(t):
             q, r = divmod(t, 2)
             var = pool.tile([P, 1], F32, name="var", bufs=2)
-            rstd[t] = pool.tile([P, 1], F32, name="rstd", bufs=2)
+            rstd[t] = pool.tile([P, 1], F32, name="rstd", bufs=4)
             nc.gpsimd.tensor_scalar(
                 out=var[:], in0=ssq[t][:], scalar1=1.0 / D, scalar2=EPS, op0=ALU.mult, op1=ALU.add
             )
             nc.gpsimd.tensor_tensor(out=rstd[t][:], in0=var[:], in1=neg_half[:], op=ALU.pow)
+
+        def normalize(t):
+            q, r = divmod(t, 2)
             z_t[t] = pool.tile([P, D], F32, name="z_t", bufs=12, align_bytes=64)
-            eng = nc.gpsimd if Z_ENGINE == "gpsimd" else nc.vector
-            eng.tensor_scalar(
-                out=z_t[t][:].rearrange("q (g t p) -> q g t p", g=2, t=4),
-                in0=mid[q][:, r, :].rearrange("q (g p t) -> q g t p", g=2, t=4),
-                scalar1=negmu[t][:],
-                scalar2=rstd[t][:],
-                op0=ALU.add,
-                op1=ALU.mult,
-            )
+            for g in range(2):
+                half = slice(g * 512, (g + 1) * 512)
+                nc.vector.tensor_scalar(
+                    out=z_t[t][:, half].rearrange("q (t h l) -> q h t l", t=4, l=4),
+                    in0=mid[q][:, r, half].rearrange("q (h l t) -> q h t l", l=4, t=4),
+                    scalar1=negmu[t][:],
+                    scalar2=rstd[t][:],
+                    op0=ALU.add,
+                    op1=ALU.mult,
+                )
 
         def store_mid(q):
             m, h = divmod(q, 2)
@@ -202,7 +205,10 @@ def tile_minitransformerlayer_pb_t_w8_kernel(
 
         def interleave(m, g):
             hgs[m, g] = pool.tile([P, GROUPS[m][1] * P, 4], BF16, name="h_group", bufs=4, align_bytes=64)
-            nc.vector.tensor_copy(out=hgs[m, g][:], in_=planes[m, g][:].rearrange("p t n -> p n t"))
+            nc.vector.tensor_copy(
+                out=hgs[m, g][:].rearrange("p (c i) t -> p c t i", i=4),
+                in_=planes[m, g][:].rearrange("p t (c i) -> p c t i", i=4),
+            )
 
         def h_quant(m, g):
             h_codes[m, g] = pool.tile([P, GROUPS[m][1] * P], U32, name="h_codes", bufs=6, align_bytes=64)
@@ -300,6 +306,8 @@ def tile_minitransformerlayer_pb_t_w8_kernel(
             if 0 <= s < TILES:
                 resid(s)
                 mean(s)
+            if 0 <= s - 2 < TILES:
+                normalize(s - 2)
             for m, g in HQ.get(s, []):
                 h_quant(m, g)
             for m, g in IL.get(s, []):

@@ -18,12 +18,18 @@ TOKENS, E, D, F = 4096, 512, 1024, 512
 TILES = TOKENS // P
 MT = 4
 MACROS = TILES // MT
-WIDTHS = [1, 1, 2] + 6 * [4] + [2, 2]
+WIDTHS = [4,4,4,4,4,4,4,2,2]
 GROUPS = [(sum(WIDTHS[:k]), w) for k, w in enumerate(WIDTHS)]
 GROUP_OF = [k for k, w in enumerate(WIDTHS) for i in range(w)]
 EPS = 1e-5
 FLOPS = 2 * TOKENS * E * D + 2 * TOKENS * D * F
-V_EVAC = ()
+V_EVAC = (7,)
+V_TAIL = 32
+PSUM_BUFS = (2,3,2)
+LAG = {"dequant":10,"a_transpose":7,"a_evac":6,"a_quant":3,"mm1":1,"square":1,"norm":6,"normalize":7,"bank":1,"affine":1,"interleave":1,"h_quant":1,"mm2":0,"gelu":2}
+RANK = ["affine","resid","gelu","norm","a_evac","a_quant","z_transpose","dequant","h_quant","square","store_mid","mean","interleave","mm1","a_transpose","store_act","normalize","mm2"]
+Z_SCALAR = (3,11,19,27)
+WARM = tuple(range(7))
 
 
 def tile_minitransformerlayer_pb_t_w8_kernel(
@@ -39,7 +45,6 @@ def tile_minitransformerlayer_pb_t_w8_kernel(
         keep = ctx.enter_context(tc.tile_pool(name="keep", bufs=1))
         pool = ctx.enter_context(tc.tile_pool(name="pool", bufs=2))
         psum = ctx.enter_context(tc.psum_pool(name="psum", bufs=2))
-        ctx.enter_context(tc.manual_schedule())
 
         ident = keep.tile([P, P], F32, name="ident")
         scale_bc = keep.tile([P, E], F32, name="scale_bc", align_bytes=64)
@@ -51,13 +56,14 @@ def tile_minitransformerlayer_pb_t_w8_kernel(
         b_raw = keep.tile([P, 2, 8], BF16, name="b_raw")
         g_col = keep.tile([P, 8], F32, name="g_col")
         b_col = keep.tile([P, 8], F32, name="b_col")
-        neg_half = keep.tile([P, 1], F32, name="neg_half")
+        neg_half = keep.tile([P, 2], F32, name="neg_half")
         warm = keep.tile([P, 1], F32, name="warm")
+        warm_bf = keep.tile([P, 512], BF16, name="warm_bf", align_bytes=64)
         sq_dump = keep.tile([P, D], BF16, name="sq_dump")
 
         a_bytes, x_t, a_bf, a_codes, a_scales = {}, {}, {}, {}, {}
         groups, mid, sums, negmu, ssq, rstd, z_t = {}, {}, {}, {}, {}, {}, {}
-        mm1_ps, planes, hgs, h_codes, h_scales, mm2_ps, act_t, zps, aps = {}, {}, {}, {}, {}, {}, {}, {}, {}
+        nbias, mm1_ps, planes, hgs, h_codes, h_scales, mm2_ps, act_t, zps, aps = {}, {}, {}, {}, {}, {}, {}, {}, {}, {}
 
         def load_a(m):
             a_bytes[m] = pool.tile([P, MT, E], U8, name="a_bytes", bufs=4, align_bytes=64)
@@ -99,7 +105,7 @@ def tile_minitransformerlayer_pb_t_w8_kernel(
             cols = slice(i * P, (i + 1) * P)
             for c in range(2):
                 n = slice(c * 512, (c + 1) * 512)
-                mm1_ps[t, c] = psum.tile([P, 512], F32, name="mm1_ps", bufs=3)
+                mm1_ps[t, c] = psum.tile([P, 512], F32, name="mm1_ps", bufs=PSUM_BUFS[0])
                 nc.tensor.matmul_mx(
                     out=mm1_ps[t, c][:],
                     lhsT=a_codes[q][:, cols].bitcast(FP8X4),
@@ -114,7 +120,7 @@ def tile_minitransformerlayer_pb_t_w8_kernel(
             m, i = divmod(t, MT)
             q, r = divmod(t, 2)
             if r == 0:
-                mid[q] = pool.tile([P, 2, D], F32, name="mid", bufs=4, align_bytes=64)
+                mid[q] = pool.tile([P, 2, D], F32, name="mid", bufs=5, align_bytes=64)
             sums[t] = pool.tile([P, 2], F32, name="sums", bufs=4)
             for c in range(2):
                 n = slice(c * 512, (c + 1) * 512)
@@ -129,8 +135,8 @@ def tile_minitransformerlayer_pb_t_w8_kernel(
                 )
 
         def mean(t):
-            negmu[t] = pool.tile([P, 1], F32, name="negmu", bufs=4)
-            nc.gpsimd.tensor_scalar(
+            negmu[t] = pool.tile([P, 1], F32, name="negmu", bufs=12)
+            nc.vector.tensor_scalar(
                 out=negmu[t][:],
                 in0=sums[t][:, 0:1],
                 scalar1=sums[t][:, 1:2],
@@ -141,30 +147,43 @@ def tile_minitransformerlayer_pb_t_w8_kernel(
 
         def square(t):
             q, r = divmod(t, 2)
-            ssq[t] = pool.tile([P, 1], F32, name="ssq", bufs=4)
+            if r == 0:
+                ssq[q] = pool.tile([P, 2], F32, name="ssq", bufs=3)
             nc.scalar.activation(
-                out=sq_dump[:], in_=mid[q][:, r, :], func=ACT.Square, bias=negmu[t][:], accum_out=ssq[t][:]
+                out=sq_dump[:], in_=mid[q][:, r, :], func=ACT.Square, bias=negmu[t][:], accum_out=ssq[q][:, r : r + 1]
             )
 
-        def norm(t):
-            q, r = divmod(t, 2)
-            var = pool.tile([P, 1], F32, name="var", bufs=2)
-            rstd[t] = pool.tile([P, 1], F32, name="rstd", bufs=4)
+        def norm(q):
+            var = pool.tile([P, 2], F32, name="var", bufs=2)
+            rstd[q] = pool.tile([P, 2], F32, name="rstd", bufs=3)
             nc.gpsimd.tensor_scalar(
-                out=var[:], in0=ssq[t][:], scalar1=1.0 / D, scalar2=EPS, op0=ALU.mult, op1=ALU.add
+                out=var[:], in0=ssq[q][:], scalar1=1.0 / D, scalar2=EPS, op0=ALU.mult, op1=ALU.add
             )
-            nc.gpsimd.tensor_tensor(out=rstd[t][:], in0=var[:], in1=neg_half[:], op=ALU.pow)
+            nc.gpsimd.tensor_tensor(out=rstd[q][:], in0=var[:], in1=neg_half[:], op=ALU.pow)
+            nbias[q] = pool.tile([P, 2], F32, name="nbias", bufs=3)
+            for r in range(2):
+                if (2 * q + r) in Z_SCALAR:
+                    nc.gpsimd.tensor_tensor(
+                        out=nbias[q][:, r : r + 1], in0=negmu[2 * q + r][:], in1=rstd[q][:, r : r + 1], op=ALU.mult
+                    )
 
         def normalize(t):
             q, r = divmod(t, 2)
             z_t[t] = pool.tile([P, D], F32, name="z_t", bufs=12, align_bytes=64)
             for g in range(2):
                 half = slice(g * 512, (g + 1) * 512)
+                dst = z_t[t][:, half].rearrange("q (t h l) -> q h t l", t=4, l=4)
+                src = mid[q][:, r, half].rearrange("q (h l t) -> q h t l", l=4, t=4)
+                if t in Z_SCALAR:
+                    nc.scalar.activation(
+                        out=dst, in_=src, func=ACT.Identity, scale=rstd[q][:, r : r + 1], bias=nbias[q][:, r : r + 1]
+                    )
+                    continue
                 nc.vector.tensor_scalar(
-                    out=z_t[t][:, half].rearrange("q (t h l) -> q h t l", t=4, l=4),
-                    in0=mid[q][:, r, half].rearrange("q (h l t) -> q h t l", l=4, t=4),
+                    out=dst,
+                    in0=src,
                     scalar1=negmu[t][:],
-                    scalar2=rstd[t][:],
+                    scalar2=rstd[q][:, r : r + 1],
                     op0=ALU.add,
                     op1=ALU.mult,
                 )
@@ -175,7 +194,9 @@ def tile_minitransformerlayer_pb_t_w8_kernel(
 
         def z_transpose(m, j):
             first, w = GROUPS[m]
-            zps[m, j] = psum.tile([P, w * P], F32, name="z_ps", bufs=2)
+            zps[m, j] = psum.tile([P, w * P], F32, name="z_ps", bufs=PSUM_BUFS[1])
+            if w == 4 and j in WARM:
+                nc.tensor.matmul(zps[m, j][:], lhsT=warm_bf[:, 0:P], rhs=warm_bf[:], start=True, stop=True)
             for i in range(w):
                 nc.tensor.transpose(
                     zps[m, j][:, i * P : (i + 1) * P], z_t[first + i][:, j * P : (j + 1) * P], ident[:]
@@ -223,7 +244,7 @@ def tile_minitransformerlayer_pb_t_w8_kernel(
             m = GROUP_OF[t]
             i = t - GROUPS[m][0]
             cols = slice(i * P, (i + 1) * P)
-            mm2_ps[t] = psum.tile([P, F], F32, name="mm2_ps", bufs=2)
+            mm2_ps[t] = psum.tile([P, F], F32, name="mm2_ps", bufs=PSUM_BUFS[2])
             for g in range(2):
                 nc.tensor.matmul_mx(
                     out=mm2_ps[t][:],
@@ -249,6 +270,7 @@ def tile_minitransformerlayer_pb_t_w8_kernel(
         nc.vector.memset(w2_scales[:].rearrange("p g n -> p (g n)").bitcast(I32), 0)
         nc.vector.memset(neg_half[:], -0.5)
         nc.vector.memset(warm[:], 0.0)
+        nc.vector.memset(warm_bf[:], 0.0)
         make_identity(nc, ident[:])
         nc.scalar.activation(out=warm[:], in_=warm[:], func=ACT.Gelu)
 
@@ -278,57 +300,53 @@ def tile_minitransformerlayer_pb_t_w8_kernel(
         nc.gpsimd.tensor_copy(out=g_col[:].rearrange("p (g t) -> p g t", g=2), in_=gb_raw[:, :, 0:4])
         nc.gpsimd.tensor_copy(out=b_col[:].rearrange("p (g t) -> p g t", g=2), in_=b_raw[:, :, 0:4])
 
-        BANKS, IL, HQ, MM2 = {}, {}, {}, {}
+        jobs = []
+
+        def add(step, stage, *args):
+            jobs.append((step, RANK.index(stage), len(jobs), args))
+
+        for t in range(TILES):
+            q, r = divmod(t, 2)
+            add(t - LAG["dequant"], "dequant", t)
+            if r == 1:
+                add(t - LAG["a_transpose"], "a_transpose", q)
+                add(t - LAG["a_evac"], "a_evac", q)
+                add(t - LAG["a_quant"], "a_quant", q)
+                add(t + LAG["norm"], "norm", q)
+                add(t, "store_mid", q)
+            add(t - LAG["mm1"], "mm1", t)
+            add(t, "resid", t)
+            add(t, "mean", t)
+            add(t + LAG["square"], "square", t)
+            add(t + LAG["normalize"], "normalize", t)
         for k, (first, w) in enumerate(GROUPS):
-            s0 = first + w + 2
+            s0 = first + w - 1 + LAG["normalize"] + LAG["bank"]
             for j in range(8):
-                BANKS.setdefault(s0 + j * w // 8, []).append((k, j))
+                add(s0 + j * w // 8, "z_transpose", k, j)
+                add(s0 + j * w // 8 + LAG["affine"], "affine", k, j, j in V_EVAC or (first >= V_TAIL and j % 2 == 1))
             ends = ((w + 1) // 2, w)
             for g in range(2):
-                IL.setdefault(s0 + ends[g] + 1, []).append((k, g))
-                HQ.setdefault(s0 + ends[g] + 2, []).append((k, g))
+                il = s0 + ends[g] - 1 + LAG["affine"] + LAG["interleave"]
+                add(il, "interleave", k, g)
+                add(il + LAG["h_quant"], "h_quant", k, g)
             for i in range(w):
-                MM2.setdefault(s0 + w + 3 + i, []).append(first + i)
-        for s in range(-6, TILES + 20):
-            if 0 <= s < TILES and s % MT == 0 and s // MT + 3 < MACROS:
-                load_a(s // MT + 3)
-            if 0 <= s < TILES and s % MT == 0 and s // MT + 2 < MACROS:
-                load_x(s // MT + 2)
-            if 0 <= s - 2 < TILES:
-                norm(s - 2)
-            q, r = divmod(s + 4, 2)
-            if r == 0 and 0 <= q < TILES // 2:
-                a_transpose(q)
-            if 0 <= s + 1 < TILES:
-                mm1(s + 1)
-            for t in MM2.get(s, []):
-                mm2(t)
-            if 0 <= s < TILES:
-                resid(s)
-                mean(s)
-            if 0 <= s - 2 < TILES:
-                normalize(s - 2)
-            for m, g in HQ.get(s, []):
-                h_quant(m, g)
-            for m, g in IL.get(s, []):
-                interleave(m, g)
-            q, r = divmod(s + 3, 2)
-            if r == 0 and 0 <= q < TILES // 2:
-                a_evac(q)
-            for m, j in BANKS.get(s - 1, []):
-                affine(m, j, j in V_EVAC or (GROUPS[m][0] >= 28 and j % 2 == 1))
-            for m, j in BANKS.get(s, []):
-                z_transpose(m, j)
-            if 0 <= s - 1 < TILES:
-                square(s - 1)
-            for t in MM2.get(s - 1, []):
-                gelu(t)
-            if 0 <= s + 6 < TILES:
-                dequant(s + 6)
-            if r == 0 and 0 <= q < TILES // 2:
-                a_quant(q)
-            if s % 2 == 1 and 0 <= s < TILES:
-                store_mid(s // 2)
-            for t in MM2.get(s - 1, []):
-                if t % 2 == 1:
-                    store_act(t // 2)
+                step = il + LAG["h_quant"] + LAG["mm2"] + i
+                add(step, "mm2", first + i)
+                add(step + LAG["gelu"], "gelu", first + i)
+                if (first + i) % 2 == 1:
+                    add(step + LAG["gelu"], "store_act", (first + i) // 2)
+        stages = {
+            "dequant": dequant, "a_transpose": a_transpose, "a_evac": a_evac, "a_quant": a_quant, "mm1": mm1,
+            "resid": resid, "mean": mean, "square": square, "norm": norm, "normalize": normalize,
+            "z_transpose": z_transpose, "affine": affine, "interleave": interleave, "h_quant": h_quant,
+            "mm2": mm2, "gelu": gelu, "store_mid": store_mid, "store_act": store_act,
+        }
+        loaded = 0
+        for step, rank, serial, args in sorted(jobs):
+            while loaded <= step // MT and loaded < MACROS:
+                if loaded + 3 < MACROS:
+                    load_a(loaded + 3)
+                if loaded + 2 < MACROS:
+                    load_x(loaded + 2)
+                loaded += 1
+            stages[RANK[rank]](*args)

@@ -18,18 +18,18 @@ TOKENS, E, D, F = 4096, 512, 1024, 512
 TILES = TOKENS // P
 MT = 4
 MACROS = TILES // MT
-WIDTHS = [4,4,4,4,4,4,4,2,2]
+WIDTHS = [4,4,4,4,4,4,4,4]
 GROUPS = [(sum(WIDTHS[:k]), w) for k, w in enumerate(WIDTHS)]
 GROUP_OF = [k for k, w in enumerate(WIDTHS) for i in range(w)]
 EPS = 1e-5
 FLOPS = 2 * TOKENS * E * D + 2 * TOKENS * D * F
-V_EVAC = (7,)
+V_EVAC = ()
 V_TAIL = 32
 PSUM_BUFS = (2,3,2)
-LAG = {"dequant":10,"a_transpose":7,"a_evac":6,"a_quant":3,"mm1":1,"square":1,"norm":6,"normalize":7,"bank":1,"affine":1,"interleave":1,"h_quant":1,"mm2":0,"gelu":2}
-RANK = ["affine","resid","gelu","norm","a_evac","a_quant","z_transpose","dequant","h_quant","square","store_mid","mean","interleave","mm1","a_transpose","store_act","normalize","mm2"]
-Z_SCALAR = (3,11,19,27)
-WARM = tuple(range(7))
+LAG = {"dequant":10,"a_transpose":9,"a_evac":7,"a_quant":5,"mm1":2,"mean":0,"square":1,"norm":3,"normalize":4,"bank":0,"affine":1,"interleave":8,"h_quant":0,"mm2":2,"gelu":1}
+RANK = ["gelu","interleave","resid","a_quant","norm","mean","store_act","mm2","store_mid","normalize","z_transpose","a_evac","affine","h_quant","square","mm1","a_transpose","dequant"]
+Z_SCALAR = (2,7,12,17,22)
+WARM = tuple(range(6))
 
 
 def tile_minitransformerlayer_pb_t_w8_kernel(
@@ -45,9 +45,10 @@ def tile_minitransformerlayer_pb_t_w8_kernel(
         keep = ctx.enter_context(tc.tile_pool(name="keep", bufs=1))
         pool = ctx.enter_context(tc.tile_pool(name="pool", bufs=2))
         psum = ctx.enter_context(tc.psum_pool(name="psum", bufs=2))
+        ctx.enter_context(tc.manual_schedule())
 
         ident = keep.tile([P, P], F32, name="ident")
-        scale_bc = keep.tile([P, E], F32, name="scale_bc", align_bytes=64)
+        scale_bc = keep.tile([P, 2 * E], F32, name="scale_bc", align_bytes=64)
         w1_words = keep.tile([P, D], I32, name="w1_words", align_bytes=64)
         w1_scales = keep.tile([P, D], U8, name="w1_scales", align_bytes=64)
         w2_words = keep.tile([P, 2, F], I32, name="w2_words", align_bytes=64)
@@ -67,25 +68,29 @@ def tile_minitransformerlayer_pb_t_w8_kernel(
 
         def load_a(m):
             a_bytes[m] = pool.tile([P, MT, E], U8, name="a_bytes", bufs=4, align_bytes=64)
-            nc.sync.dma_start(out=a_bytes[m][:], in_=bytes_v[m])
+            for h in range(2):
+                nc.sync.dma_start(out=a_bytes[m][:, 2 * h : 2 * h + 2, :], in_=bytes_v[m][:, 2 * h : 2 * h + 2, :])
 
         def load_x(m):
             x_t[m] = pool.tile([P, MT, D], BF16, name="x_t", bufs=3, align_bytes=64)
             for h in range(2):
                 nc.sync.dma_start(out=x_t[m][:, 2 * h : 2 * h + 2, :], in_=x_v[m][:, 2 * h : 2 * h + 2, :])
 
-        def dequant(t):
-            m, i = divmod(t, MT)
-            a_bf[t] = pool.tile([P, E], BF16, name="a_bf", bufs=5, align_bytes=64)
+        def dequant(q):
+            m, h = divmod(q, 2)
+            a_bf[q] = pool.tile([P, 2 * E], BF16, name="a_bf", bufs=3, align_bytes=64)
             nc.vector.tensor_tensor(
-                out=a_bf[t][:], in0=a_bytes[m][:, i, :].bitcast(FP8), in1=scale_bc[:], op=ALU.mult
+                out=a_bf[q][:],
+                in0=a_bytes[m][:, 2 * h : 2 * h + 2, :].rearrange("p i k -> p (i k)").bitcast(FP8),
+                in1=scale_bc[:],
+                op=ALU.mult,
             )
 
         def a_transpose(q):
             aps[q] = psum.tile([P, 4, P], F32, name="a_ps", bufs=1)
             for i in range(2):
-                words = a_bf[2 * q + i][:].bitcast(F32)
                 for u in range(2):
+                    words = a_bf[q][:, i * E : (i + 1) * E].bitcast(F32)
                     nc.tensor.transpose(aps[q][:, 2 * i + u, :], words[:, u : E // 2 : 2], ident[:])
 
         def a_evac(q):
@@ -121,7 +126,8 @@ def tile_minitransformerlayer_pb_t_w8_kernel(
             q, r = divmod(t, 2)
             if r == 0:
                 mid[q] = pool.tile([P, 2, D], F32, name="mid", bufs=5, align_bytes=64)
-            sums[t] = pool.tile([P, 2], F32, name="sums", bufs=4)
+            if r == 0:
+                sums[q] = pool.tile([P, 2, 2], F32, name="sums", bufs=4)
             for c in range(2):
                 n = slice(c * 512, (c + 1) * 512)
                 nc.vector.scalar_tensor_tensor(
@@ -131,18 +137,15 @@ def tile_minitransformerlayer_pb_t_w8_kernel(
                     in1=x_t[m][:, i, n],
                     op0=ALU.mult,
                     op1=ALU.add,
-                    accum_out=sums[t][:, c : c + 1],
+                    accum_out=sums[q][:, c, r : r + 1],
                 )
 
-        def mean(t):
-            negmu[t] = pool.tile([P, 1], F32, name="negmu", bufs=12)
-            nc.vector.tensor_scalar(
-                out=negmu[t][:],
-                in0=sums[t][:, 0:1],
-                scalar1=sums[t][:, 1:2],
-                scalar2=-1.0 / D,
-                op0=ALU.add,
-                op1=ALU.mult,
+        def mean(q):
+            total = pool.tile([P, 2], F32, name="total", bufs=2)
+            negmu[q] = pool.tile([P, 2], F32, name="negmu", bufs=6)
+            nc.gpsimd.tensor_tensor(out=total[:], in0=sums[q][:, 0, :], in1=sums[q][:, 1, :], op=ALU.add)
+            nc.gpsimd.tensor_scalar(
+                out=negmu[q][:], in0=total[:], scalar1=-1.0 / D, scalar2=0.0, op0=ALU.mult, op1=ALU.add
             )
 
         def square(t):
@@ -150,7 +153,7 @@ def tile_minitransformerlayer_pb_t_w8_kernel(
             if r == 0:
                 ssq[q] = pool.tile([P, 2], F32, name="ssq", bufs=3)
             nc.scalar.activation(
-                out=sq_dump[:], in_=mid[q][:, r, :], func=ACT.Square, bias=negmu[t][:], accum_out=ssq[q][:, r : r + 1]
+                out=sq_dump[:], in_=mid[q][:, r, :], func=ACT.Square, bias=negmu[q][:, r : r + 1], accum_out=ssq[q][:, r : r + 1]
             )
 
         def norm(q):
@@ -164,25 +167,23 @@ def tile_minitransformerlayer_pb_t_w8_kernel(
             for r in range(2):
                 if (2 * q + r) in Z_SCALAR:
                     nc.gpsimd.tensor_tensor(
-                        out=nbias[q][:, r : r + 1], in0=negmu[2 * q + r][:], in1=rstd[q][:, r : r + 1], op=ALU.mult
+                        out=nbias[q][:, r : r + 1], in0=negmu[q][:, r : r + 1], in1=rstd[q][:, r : r + 1], op=ALU.mult
                     )
 
         def normalize(t):
             q, r = divmod(t, 2)
             z_t[t] = pool.tile([P, D], F32, name="z_t", bufs=12, align_bytes=64)
-            for g in range(2):
-                half = slice(g * 512, (g + 1) * 512)
-                dst = z_t[t][:, half].rearrange("q (t h l) -> q h t l", t=4, l=4)
-                src = mid[q][:, r, half].rearrange("q (h l t) -> q h t l", l=4, t=4)
-                if t in Z_SCALAR:
-                    nc.scalar.activation(
-                        out=dst, in_=src, func=ACT.Identity, scale=rstd[q][:, r : r + 1], bias=nbias[q][:, r : r + 1]
-                    )
-                    continue
+            dst = z_t[t][:].rearrange("q (g t p) -> q g p t", g=2, t=4)
+            src = mid[q][:, r, :].rearrange("q (g p t) -> q g p t", g=2, t=4)
+            if t in Z_SCALAR:
+                nc.scalar.activation(
+                    out=dst, in_=src, func=ACT.Identity, scale=rstd[q][:, r : r + 1], bias=nbias[q][:, r : r + 1]
+                )
+            else:
                 nc.vector.tensor_scalar(
                     out=dst,
                     in0=src,
-                    scalar1=negmu[t][:],
+                    scalar1=negmu[q][:, r : r + 1],
                     scalar2=rstd[q][:, r : r + 1],
                     op0=ALU.add,
                     op1=ALU.mult,
@@ -195,8 +196,8 @@ def tile_minitransformerlayer_pb_t_w8_kernel(
         def z_transpose(m, j):
             first, w = GROUPS[m]
             zps[m, j] = psum.tile([P, w * P], F32, name="z_ps", bufs=PSUM_BUFS[1])
-            if w == 4 and j in WARM:
-                nc.tensor.matmul(zps[m, j][:], lhsT=warm_bf[:, 0:P], rhs=warm_bf[:], start=True, stop=True)
+            if j in WARM:
+                nc.tensor.matmul(zps[m, j][:], lhsT=warm_bf[:, 0:P], rhs=warm_bf[:, 0 : w * P], start=True, stop=True)
             for i in range(w):
                 nc.tensor.transpose(
                     zps[m, j][:, i * P : (i + 1) * P], z_t[first + i][:, j * P : (j + 1) * P], ident[:]
@@ -274,7 +275,7 @@ def tile_minitransformerlayer_pb_t_w8_kernel(
         make_identity(nc, ident[:])
         nc.scalar.activation(out=warm[:], in_=warm[:], func=ACT.Gelu)
 
-        nc.sync.dma_start(out=scale_bc[:], in_=h_attn_scale.rearrange("a b k -> (a b k)").partition_broadcast(P))
+        nc.sync.dma_start(out=scale_bc[:, 0:E], in_=h_attn_scale.rearrange("a b k -> (a b k)").partition_broadcast(P))
         load_a(0)
         nc.sync.dma_start(out=w1_words[:], in_=w_out_words[0].rearrange("p n t -> p (n t)").bitcast(I32))
         s1 = w_out_scales[0].bitcast(I32)
@@ -300,6 +301,8 @@ def tile_minitransformerlayer_pb_t_w8_kernel(
         nc.gpsimd.tensor_copy(out=g_col[:].rearrange("p (g t) -> p g t", g=2), in_=gb_raw[:, :, 0:4])
         nc.gpsimd.tensor_copy(out=b_col[:].rearrange("p (g t) -> p g t", g=2), in_=b_raw[:, :, 0:4])
 
+        nc.vector.tensor_copy(out=scale_bc[:, E : 2 * E], in_=scale_bc[:, 0:E])
+
         jobs = []
 
         def add(step, stage, *args):
@@ -307,8 +310,9 @@ def tile_minitransformerlayer_pb_t_w8_kernel(
 
         for t in range(TILES):
             q, r = divmod(t, 2)
-            add(t - LAG["dequant"], "dequant", t)
             if r == 1:
+                add(t - LAG["dequant"], "dequant", q)
+                add(t + LAG["mean"], "mean", q)
                 add(t - LAG["a_transpose"], "a_transpose", q)
                 add(t - LAG["a_evac"], "a_evac", q)
                 add(t - LAG["a_quant"], "a_quant", q)
@@ -316,7 +320,6 @@ def tile_minitransformerlayer_pb_t_w8_kernel(
                 add(t, "store_mid", q)
             add(t - LAG["mm1"], "mm1", t)
             add(t, "resid", t)
-            add(t, "mean", t)
             add(t + LAG["square"], "square", t)
             add(t + LAG["normalize"], "normalize", t)
         for k, (first, w) in enumerate(GROUPS):

@@ -26,10 +26,10 @@ FLOPS = 2 * TOKENS * E * D + 2 * TOKENS * D * F
 V_EVAC = ()
 V_TAIL = 32
 PSUM_BUFS = (2,3,2)
-LAG = {"dequant":10,"a_transpose":9,"a_evac":7,"a_quant":5,"mm1":2,"mean":0,"square":1,"norm":3,"normalize":4,"bank":0,"affine":1,"interleave":8,"h_quant":0,"mm2":2,"gelu":1}
-RANK = ["gelu","interleave","resid","a_quant","norm","mean","store_act","mm2","store_mid","normalize","z_transpose","a_evac","affine","h_quant","square","mm1","a_transpose","dequant"]
-Z_SCALAR = (2,7,12,17,22)
-WARM = tuple(range(6))
+LAG = {"dequant":9,"a_transpose":7,"a_evac":6,"a_quant":4,"mm1":2,"mean":0,"square":1,"norm":2,"normalize":5,"bank":0,"affine":1,"interleave":4,"h_quant":0,"mm2":1,"gelu":1,"var":2,"shift":4}
+RANK = ["resid","a_evac","a_quant","normalize","gelu","a_transpose","interleave","dequant","mm2","store_mid","z_transpose","mean","var","store_act","shift","h_quant","affine","norm","square","mm1"]
+Z_SCALAR = (1,3,5,7,9,11,13,15,17)
+WARM = (0, 2, 4, 6)
 
 
 def tile_minitransformerlayer_pb_t_w8_kernel(
@@ -64,7 +64,7 @@ def tile_minitransformerlayer_pb_t_w8_kernel(
 
         a_bytes, x_t, a_bf, a_codes, a_scales = {}, {}, {}, {}, {}
         groups, mid, sums, negmu, ssq, rstd, z_t = {}, {}, {}, {}, {}, {}, {}
-        nbias, mm1_ps, planes, hgs, h_codes, h_scales, mm2_ps, act_t, zps, aps = {}, {}, {}, {}, {}, {}, {}, {}, {}, {}
+        nbias, var_t, mm1_ps, planes, hgs, h_codes, h_scales, mm2_ps, act_t, zps, aps = {}, {}, {}, {}, {}, {}, {}, {}, {}, {}, {}
 
         def load_a(m):
             a_bytes[m] = pool.tile([P, MT, E], U8, name="a_bytes", bufs=4, align_bytes=64)
@@ -125,7 +125,7 @@ def tile_minitransformerlayer_pb_t_w8_kernel(
             m, i = divmod(t, MT)
             q, r = divmod(t, 2)
             if r == 0:
-                mid[q] = pool.tile([P, 2, D], F32, name="mid", bufs=5, align_bytes=64)
+                mid[q] = pool.tile([P, 2, D], F32, name="mid", bufs=6, align_bytes=64)
             if r == 0:
                 sums[q] = pool.tile([P, 2, 2], F32, name="sums", bufs=4)
             for c in range(2):
@@ -140,12 +140,17 @@ def tile_minitransformerlayer_pb_t_w8_kernel(
                     accum_out=sums[q][:, c, r : r + 1],
                 )
 
-        def mean(q):
-            total = pool.tile([P, 2], F32, name="total", bufs=2)
-            negmu[q] = pool.tile([P, 2], F32, name="negmu", bufs=6)
-            nc.gpsimd.tensor_tensor(out=total[:], in0=sums[q][:, 0, :], in1=sums[q][:, 1, :], op=ALU.add)
-            nc.gpsimd.tensor_scalar(
-                out=negmu[q][:], in0=total[:], scalar1=-1.0 / D, scalar2=0.0, op0=ALU.mult, op1=ALU.add
+        def mean(t):
+            q, r = divmod(t, 2)
+            if r == 0:
+                negmu[q] = pool.tile([P, 2], F32, name="negmu", bufs=6)
+            nc.vector.tensor_scalar(
+                out=negmu[q][:, r : r + 1],
+                in0=sums[q][:, 0, r : r + 1],
+                scalar1=sums[q][:, 1, r : r + 1],
+                scalar2=-1.0 / D,
+                op0=ALU.add,
+                op1=ALU.mult,
             )
 
         def square(t):
@@ -156,38 +161,45 @@ def tile_minitransformerlayer_pb_t_w8_kernel(
                 out=sq_dump[:], in_=mid[q][:, r, :], func=ACT.Square, bias=negmu[q][:, r : r + 1], accum_out=ssq[q][:, r : r + 1]
             )
 
-        def norm(q):
-            var = pool.tile([P, 2], F32, name="var", bufs=2)
-            rstd[q] = pool.tile([P, 2], F32, name="rstd", bufs=3)
-            nc.gpsimd.tensor_scalar(
-                out=var[:], in0=ssq[q][:], scalar1=1.0 / D, scalar2=EPS, op0=ALU.mult, op1=ALU.add
+        def var(q):
+            var_t[q] = pool.tile([P, 2], F32, name="var", bufs=2)
+            nc.vector.tensor_scalar(
+                out=var_t[q][:], in0=ssq[q][:], scalar1=1.0 / D, scalar2=EPS, op0=ALU.mult, op1=ALU.add
             )
-            nc.gpsimd.tensor_tensor(out=rstd[q][:], in0=var[:], in1=neg_half[:], op=ALU.pow)
-            nbias[q] = pool.tile([P, 2], F32, name="nbias", bufs=3)
-            for r in range(2):
-                if (2 * q + r) in Z_SCALAR:
-                    nc.gpsimd.tensor_tensor(
-                        out=nbias[q][:, r : r + 1], in0=negmu[q][:, r : r + 1], in1=rstd[q][:, r : r + 1], op=ALU.mult
-                    )
+
+        def norm(q):
+            rstd[q] = pool.tile([P, 2], F32, name="rstd", bufs=4)
+            nc.gpsimd.tensor_tensor(out=rstd[q][:], in0=var_t[q][:], in1=neg_half[:], op=ALU.pow)
+
+        def shift(t):
+            q, r = divmod(t, 2)
+            nbias[t] = pool.tile([P, 1], F32, name="nbias", bufs=3)
+            nc.vector.tensor_scalar(
+                out=nbias[t][:],
+                in0=negmu[q][:, r : r + 1],
+                scalar1=rstd[q][:, r : r + 1],
+                scalar2=None,
+                op0=ALU.mult,
+            )
 
         def normalize(t):
             q, r = divmod(t, 2)
-            z_t[t] = pool.tile([P, D], F32, name="z_t", bufs=12, align_bytes=64)
+            z_t[t] = pool.tile([P, D], F32, name="z_t", bufs=11, align_bytes=64)
             dst = z_t[t][:].rearrange("q (g t p) -> q g p t", g=2, t=4)
             src = mid[q][:, r, :].rearrange("q (g p t) -> q g p t", g=2, t=4)
-            if t in Z_SCALAR:
+            split = 1 if t in Z_SCALAR else 2
+            if split == 1:
                 nc.scalar.activation(
-                    out=dst, in_=src, func=ACT.Identity, scale=rstd[q][:, r : r + 1], bias=nbias[q][:, r : r + 1]
+                    out=dst[:, 1], in_=src[:, 1], func=ACT.Identity, scale=rstd[q][:, r : r + 1], bias=nbias[t][:]
                 )
-            else:
-                nc.vector.tensor_scalar(
-                    out=dst,
-                    in0=src,
-                    scalar1=negmu[q][:, r : r + 1],
-                    scalar2=rstd[q][:, r : r + 1],
-                    op0=ALU.add,
-                    op1=ALU.mult,
-                )
+            nc.vector.tensor_scalar(
+                out=dst[:, 0:split],
+                in0=src[:, 0:split],
+                scalar1=negmu[q][:, r : r + 1],
+                scalar2=rstd[q][:, r : r + 1],
+                op0=ALU.add,
+                op1=ALU.mult,
+            )
 
         def store_mid(q):
             m, h = divmod(q, 2)
@@ -260,7 +272,7 @@ def tile_minitransformerlayer_pb_t_w8_kernel(
         def gelu(t):
             q, r = divmod(t, 2)
             if r == 0:
-                act_t[q] = pool.tile([P, 2, F], F32, name="act_t", bufs=6, align_bytes=64)
+                act_t[q] = pool.tile([P, 2, F], F32, name="act_t", bufs=5, align_bytes=64)
             nc.scalar.activation(out=act_t[q][:, r, :], in_=mm2_ps[t][:], func=ACT.Gelu)
 
         def store_act(q):
@@ -312,15 +324,18 @@ def tile_minitransformerlayer_pb_t_w8_kernel(
             q, r = divmod(t, 2)
             if r == 1:
                 add(t - LAG["dequant"], "dequant", q)
-                add(t + LAG["mean"], "mean", q)
                 add(t - LAG["a_transpose"], "a_transpose", q)
                 add(t - LAG["a_evac"], "a_evac", q)
                 add(t - LAG["a_quant"], "a_quant", q)
+                add(t + LAG["var"], "var", q)
                 add(t + LAG["norm"], "norm", q)
                 add(t, "store_mid", q)
             add(t - LAG["mm1"], "mm1", t)
             add(t, "resid", t)
+            add(t + LAG["mean"], "mean", t)
             add(t + LAG["square"], "square", t)
+            if t in Z_SCALAR:
+                add(t + LAG["shift"], "shift", t)
             add(t + LAG["normalize"], "normalize", t)
         for k, (first, w) in enumerate(GROUPS):
             s0 = first + w - 1 + LAG["normalize"] + LAG["bank"]
@@ -340,7 +355,7 @@ def tile_minitransformerlayer_pb_t_w8_kernel(
                     add(step + LAG["gelu"], "store_act", (first + i) // 2)
         stages = {
             "dequant": dequant, "a_transpose": a_transpose, "a_evac": a_evac, "a_quant": a_quant, "mm1": mm1,
-            "resid": resid, "mean": mean, "square": square, "norm": norm, "normalize": normalize,
+            "resid": resid, "mean": mean, "square": square, "var": var, "norm": norm, "shift": shift, "normalize": normalize,
             "z_transpose": z_transpose, "affine": affine, "interleave": interleave, "h_quant": h_quant,
             "mm2": mm2, "gelu": gelu, "store_mid": store_mid, "store_act": store_act,
         }

from contextlib import ExitStack

import concourse.mybir as mybir
from concourse.masks import make_identity

F32 = mybir.dt.float32
BF16 = mybir.dt.bfloat16
I32 = mybir.dt.int32
U32 = mybir.dt.uint32
U8 = mybir.dt.uint8
FP8 = mybir.dt.float8_e4m3fn
FP8X4 = mybir.dt.float8_e4m3fn_x4
ALU = mybir.AluOpType
ACT = mybir.ActivationFunctionType

P = 128
TOKENS, E, D, F = 4096, 512, 1024, 512
TILES = TOKENS // P
MT = 4
MACROS = TILES // MT
WIDTHS = [4,4,4,4,4,4,4,4]
GROUPS = [(sum(WIDTHS[:k]), w) for k, w in enumerate(WIDTHS)]
GROUP_OF = [k for k, w in enumerate(WIDTHS) for i in range(w)]
EPS = 1e-5
FLOPS = 2 * TOKENS * E * D + 2 * TOKENS * D * F
V_EVAC = ()
V_TAIL = 32
PSUM_BUFS = (2,3,2)
LAG = {"dequant":9,"a_transpose":7,"a_evac":6,"a_quant":4,"mm1":2,"mean":0,"square":1,"norm":2,"normalize":5,"bank":0,"affine":1,"interleave":4,"h_quant":0,"mm2":1,"gelu":1,"var":2,"shift":4}
RANK = ["resid","a_evac","a_quant","normalize","gelu","a_transpose","interleave","dequant","mm2","store_mid","z_transpose","mean","var","store_act","shift","h_quant","affine","norm","square","mm1"]
Z_SCALAR = (1,3,5,7,9,11,13,15,17)
WARM = (0, 2, 4, 6)


def tile_minitransformerlayer_pb_t_w8_kernel(
    tc, h_attn_bytes, h_attn_scale, x, w_out_words, w_out_scales, w_fc1_words, w_fc1_scales, g2, b2, out_0, out_1
):
    nc = tc.nc
    bytes_v = h_attn_bytes.flatten_outer_dims().rearrange("(m p i) k -> m p i k", p=P, i=MT)
    x_v = x.flatten_outer_dims().rearrange("(m p i) d -> m p i d", p=P, i=MT)
    mid_v = out_0.flatten_outer_dims().rearrange("(m p i) d -> m p i d", p=P, i=MT)
    act_v = out_1.flatten_outer_dims().rearrange("(m p i) f -> m p i f", p=P, i=MT)

    with ExitStack() as ctx:
        keep = ctx.enter_context(tc.tile_pool(name="keep", bufs=1))
        pool = ctx.enter_context(tc.tile_pool(name="pool", bufs=2))
        psum = ctx.enter_context(tc.psum_pool(name="psum", bufs=2))
        ctx.enter_context(tc.manual_schedule())

        ident = keep.tile([P, P], F32, name="ident")
        scale_bc = keep.tile([P, 2 * E], F32, name="scale_bc", align_bytes=64)
        w1_words = keep.tile([P, D], I32, name="w1_words", align_bytes=64)
        w1_scales = keep.tile([P, D], U8, name="w1_scales", align_bytes=64)
        w2_words = keep.tile([P, 2, F], I32, name="w2_words", align_bytes=64)
        w2_scales = keep.tile([P, 2, F], U8, name="w2_scales", align_bytes=64)
        gb_raw = keep.tile([P, 2, 8], BF16, name="gb_raw")
        b_raw = keep.tile([P, 2, 8], BF16, name="b_raw")
        g_col = keep.tile([P, 8], F32, name="g_col")
        b_col = keep.tile([P, 8], F32, name="b_col")
        neg_half = keep.tile([P, 2], F32, name="neg_half")
        warm = keep.tile([P, 1], F32, name="warm")
        warm_bf = keep.tile([P, 512], BF16, name="warm_bf", align_bytes=64)
        sq_dump = keep.tile([P, D], BF16, name="sq_dump")

        a_bytes, x_t, a_bf, a_codes, a_scales = {}, {}, {}, {}, {}
        groups, mid, sums, negmu, ssq, rstd, z_t = {}, {}, {}, {}, {}, {}, {}
        nbias, var_t, mm1_ps, planes, hgs, h_codes, h_scales, mm2_ps, act_t, zps, aps = {}, {}, {}, {}, {}, {}, {}, {}, {}, {}, {}

        def load_a(m):
            a_bytes[m] = pool.tile([P, MT, E], U8, name="a_bytes", bufs=4, align_bytes=64)
            for h in range(2):
                nc.sync.dma_start(out=a_bytes[m][:, 2 * h : 2 * h + 2, :], in_=bytes_v[m][:, 2 * h : 2 * h + 2, :])

        def load_x(m):
            x_t[m] = pool.tile([P, MT, D], BF16, name="x_t", bufs=3, align_bytes=64)
            for h in range(2):
                nc.sync.dma_start(out=x_t[m][:, 2 * h : 2 * h + 2, :], in_=x_v[m][:, 2 * h : 2 * h + 2, :])

        def dequant(q):
            m, h = divmod(q, 2)
            a_bf[q] = pool.tile([P, 2 * E], BF16, name="a_bf", bufs=3, align_bytes=64)
            nc.vector.tensor_tensor(
                out=a_bf[q][:],
                in0=a_bytes[m][:, 2 * h : 2 * h + 2, :].rearrange("p i k -> p (i k)").bitcast(FP8),
                in1=scale_bc[:],
                op=ALU.mult,
            )

        def a_transpose(q):
            aps[q] = psum.tile([P, 4, P], F32, name="a_ps", bufs=1)
            for i in range(2):
                for u in range(2):
                    words = a_bf[q][:, i * E : (i + 1) * E].bitcast(F32)
                    nc.tensor.transpose(aps[q][:, 2 * i + u, :], words[:, u : E // 2 : 2], ident[:])

        def a_evac(q):
            groups[q] = pool.tile([P, 8 * P], BF16, name="a_group", bufs=2, align_bytes=64)
            nc.scalar.copy(
                out=groups[q][:].bitcast(F32).rearrange("p (i n u) -> p i n u", i=2, u=2),
                in_=aps[q][:].rearrange("p (i u) n -> p i n u", u=2),
            )

        def a_quant(q):
            a_codes[q] = pool.tile([P, 2 * P], U32, name="a_codes", bufs=3, align_bytes=64)
            a_scales[q] = pool.tile([P, 2 * P], U8, name="a_scales", bufs=3, align_bytes=64)
            nc.vector.quantize_mx(out=a_codes[q][:].bitcast(FP8X4), scales=a_scales[q][:], in_=groups[q][:])

        def mm1(t):
            q, i = divmod(t, 2)
            cols = slice(i * P, (i + 1) * P)
            for c in range(2):
                n = slice(c * 512, (c + 1) * 512)
                mm1_ps[t, c] = psum.tile([P, 512], F32, name="mm1_ps", bufs=PSUM_BUFS[0])
                nc.tensor.matmul_mx(
                    out=mm1_ps[t, c][:],
                    lhsT=a_codes[q][:, cols].bitcast(FP8X4),
                    lhsT_scale=a_scales[q][:, cols],
                    rhs=w1_words[:, n].bitcast(FP8X4),
                    rhs_scale=w1_scales[:, n],
                    start=True,
                    stop=True,
                )

        def resid(t):
            m, i = divmod(t, MT)
            q, r = divmod(t, 2)
            if r == 0:
                mid[q] = pool.tile([P, 2, D], F32, name="mid", bufs=6, align_bytes=64)
            if r == 0:
                sums[q] = pool.tile([P, 2, 2], F32, name="sums", bufs=4)
            for c in range(2):
                n = slice(c * 512, (c + 1) * 512)
                nc.vector.scalar_tensor_tensor(
                    out=mid[q][:, r, n],
                    in0=mm1_ps[t, c][:],
                    scalar=1.0,
                    in1=x_t[m][:, i, n],
                    op0=ALU.mult,
                    op1=ALU.add,
                    accum_out=sums[q][:, c, r : r + 1],
                )

        def mean(t):
            q, r = divmod(t, 2)
            if r == 0:
                negmu[q] = pool.tile([P, 2], F32, name="negmu", bufs=6)
            nc.vector.tensor_scalar(
                out=negmu[q][:, r : r + 1],
                in0=sums[q][:, 0, r : r + 1],
                scalar1=sums[q][:, 1, r : r + 1],
                scalar2=-1.0 / D,
                op0=ALU.add,
                op1=ALU.mult,
            )

        def square(t):
            q, r = divmod(t, 2)
            if r == 0:
                ssq[q] = pool.tile([P, 2], F32, name="ssq", bufs=3)
            nc.scalar.activation(
                out=sq_dump[:], in_=mid[q][:, r, :], func=ACT.Square, bias=negmu[q][:, r : r + 1], accum_out=ssq[q][:, r : r + 1]
            )

        def var(q):
            var_t[q] = pool.tile([P, 2], F32, name="var", bufs=2)
            nc.vector.tensor_scalar(
                out=var_t[q][:], in0=ssq[q][:], scalar1=1.0 / D, scalar2=EPS, op0=ALU.mult, op1=ALU.add
            )

        def norm(q):
            rstd[q] = pool.tile([P, 2], F32, name="rstd", bufs=4)
            nc.gpsimd.tensor_tensor(out=rstd[q][:], in0=var_t[q][:], in1=neg_half[:], op=ALU.pow)

        def shift(t):
            q, r = divmod(t, 2)
            nbias[t] = pool.tile([P, 1], F32, name="nbias", bufs=3)
            nc.vector.tensor_scalar(
                out=nbias[t][:],
                in0=negmu[q][:, r : r + 1],
                scalar1=rstd[q][:, r : r + 1],
                scalar2=None,
                op0=ALU.mult,
            )

        def normalize(t):
            q, r = divmod(t, 2)
            z_t[t] = pool.tile([P, D], F32, name="z_t", bufs=11, align_bytes=64)
            dst = z_t[t][:].rearrange("q (g t p) -> q g p t", g=2, t=4)
            src = mid[q][:, r, :].rearrange("q (g p t) -> q g p t", g=2, t=4)
            split = 1 if t in Z_SCALAR else 2
            if split == 1:
                nc.scalar.activation(
                    out=dst[:, 1], in_=src[:, 1], func=ACT.Identity, scale=rstd[q][:, r : r + 1], bias=nbias[t][:]
                )
            nc.vector.tensor_scalar(
                out=dst[:, 0:split],
                in0=src[:, 0:split],
                scalar1=negmu[q][:, r : r + 1],
                scalar2=rstd[q][:, r : r + 1],
                op0=ALU.add,
                op1=ALU.mult,
            )

        def store_mid(q):
            m, h = divmod(q, 2)
            nc.sync.dma_start(out=mid_v[m][:, 2 * h : 2 * h + 2, :], in_=mid[q][:])

        def z_transpose(m, j):
            first, w = GROUPS[m]
            zps[m, j] = psum.tile([P, w * P], F32, name="z_ps", bufs=PSUM_BUFS[1])
            if j in WARM:
                nc.tensor.matmul(zps[m, j][:], lhsT=warm_bf[:, 0:P], rhs=warm_bf[:, 0 : w * P], start=True, stop=True)
            for i in range(w):
                nc.tensor.transpose(
                    zps[m, j][:, i * P : (i + 1) * P], z_t[first + i][:, j * P : (j + 1) * P], ident[:]
                )

        def affine(m, j, on_vector):
            g, t = divmod(j, 4)
            if t == 0:
                planes[m, g] = pool.tile([P, 4, GROUPS[m][1] * P], BF16, name="planes", bufs=5, align_bytes=64)
            if on_vector:
                nc.vector.tensor_scalar(
                    out=planes[m, g][:, t, :],
                    in0=zps[m, j][:],
                    scalar1=g_col[:, j : j + 1],
                    scalar2=b_col[:, j : j + 1],
                    op0=ALU.mult,
                    op1=ALU.add,
                )
            else:
                nc.scalar.activation(
                    out=planes[m, g][:, t, :],
                    in_=zps[m, j][:],
                    func=ACT.Identity,
                    scale=g_col[:, j : j + 1],
                    bias=b_col[:, j : j + 1],
                )

        def interleave(m, g):
            hgs[m, g] = pool.tile([P, GROUPS[m][1] * P, 4], BF16, name="h_group", bufs=4, align_bytes=64)
            nc.vector.tensor_copy(
                out=hgs[m, g][:].rearrange("p (c i) t -> p c t i", i=4),
                in_=planes[m, g][:].rearrange("p t (c i) -> p c t i", i=4),
            )

        def h_quant(m, g):
            h_codes[m, g] = pool.tile([P, GROUPS[m][1] * P], U32, name="h_codes", bufs=6, align_bytes=64)
            h_scales[m, g] = pool.tile([P, GROUPS[m][1] * P], U8, name="h_scales", bufs=6, align_bytes=64)
            nc.vector.quantize_mx(
                out=h_codes[m, g][:].bitcast(FP8X4),
                scales=h_scales[m, g][:],
                in_=hgs[m, g][:].rearrange("p n t -> p (n t)"),
            )

        def mm2(t):
            m = GROUP_OF[t]
            i = t - GROUPS[m][0]
            cols = slice(i * P, (i + 1) * P)
            mm2_ps[t] = psum.tile([P, F], F32, name="mm2_ps", bufs=PSUM_BUFS[2])
            for g in range(2):
                nc.tensor.matmul_mx(
                    out=mm2_ps[t][:],
                    lhsT=h_codes[m, g][:, cols].bitcast(FP8X4),
                    lhsT_scale=h_scales[m, g][:, cols],
                    rhs=w2_words[:, g, :].bitcast(FP8X4),
                    rhs_scale=w2_scales[:, g, :],
                    start=(g == 0),
                    stop=(g == 1),
                )

        def gelu(t):
            q, r = divmod(t, 2)
            if r == 0:
                act_t[q] = pool.tile([P, 2, F], F32, name="act_t", bufs=5, align_bytes=64)
            nc.scalar.activation(out=act_t[q][:, r, :], in_=mm2_ps[t][:], func=ACT.Gelu)

        def store_act(q):
            m, h = divmod(q, 2)
            nc.sync.dma_start(out=act_v[m][:, 2 * h : 2 * h + 2, :], in_=act_t[q][:])

        nc.vector.memset(w1_scales[:].bitcast(I32), 0)
        nc.vector.memset(w2_scales[:].rearrange("p g n -> p (g n)").bitcast(I32), 0)
        nc.vector.memset(neg_half[:], -0.5)
        nc.vector.memset(warm[:], 0.0)
        nc.vector.memset(warm_bf[:], 0.0)
        make_identity(nc, ident[:])
        nc.scalar.activation(out=warm[:], in_=warm[:], func=ACT.Gelu)

        nc.sync.dma_start(out=scale_bc[:, 0:E], in_=h_attn_scale.rearrange("a b k -> (a b k)").partition_broadcast(P))
        load_a(0)
        nc.sync.dma_start(out=w1_words[:], in_=w_out_words[0].rearrange("p n t -> p (n t)").bitcast(I32))
        s1 = w_out_scales[0].bitcast(I32)
        for quad in range(4):
            nc.sync.dma_start(
                out=w1_scales[32 * quad : 32 * quad + 4, :].bitcast(I32), in_=s1[4 * quad : 4 * quad + 4, :]
            )
        load_a(1)
        load_x(0)
        nc.sync.dma_start(out=gb_raw[:, :, 0:4], in_=g2.rearrange("(g p t) -> p g t", p=P, t=4))
        nc.sync.dma_start(out=b_raw[:, :, 0:4], in_=b2.rearrange("(g p t) -> p g t", p=P, t=4))
        load_a(2)
        load_x(1)
        nc.sync.dma_start(
            out=w2_words[:],
            in_=w_fc1_words.rearrange("g p n t -> p g (n t)").bitcast(I32),
        )
        s2 = w_fc1_scales.bitcast(I32).rearrange("g q n -> q g n")
        for quad in range(4):
            nc.sync.dma_start(
                out=w2_scales[32 * quad : 32 * quad + 4, :, :].bitcast(I32), in_=s2[4 * quad : 4 * quad + 4]
            )
        nc.gpsimd.tensor_copy(out=g_col[:].rearrange("p (g t) -> p g t", g=2), in_=gb_raw[:, :, 0:4])
        nc.gpsimd.tensor_copy(out=b_col[:].rearrange("p (g t) -> p g t", g=2), in_=b_raw[:, :, 0:4])

        nc.vector.tensor_copy(out=scale_bc[:, E : 2 * E], in_=scale_bc[:, 0:E])

        jobs = []

        def add(step, stage, *args):
            jobs.append((step, RANK.index(stage), len(jobs), args))

        for t in range(TILES):
            q, r = divmod(t, 2)
            if r == 1:
                add(t - LAG["dequant"], "dequant", q)
                add(t - LAG["a_transpose"], "a_transpose", q)
                add(t - LAG["a_evac"], "a_evac", q)
                add(t - LAG["a_quant"], "a_quant", q)
                add(t + LAG["var"], "var", q)
                add(t + LAG["norm"], "norm", q)
                add(t, "store_mid", q)
            add(t - LAG["mm1"], "mm1", t)
            add(t, "resid", t)
            add(t + LAG["mean"], "mean", t)
            add(t + LAG["square"], "square", t)
            if t in Z_SCALAR:
                add(t + LAG["shift"], "shift", t)
            add(t + LAG["normalize"], "normalize", t)
        for k, (first, w) in enumerate(GROUPS):
            s0 = first + w - 1 + LAG["normalize"] + LAG["bank"]
            for j in range(8):
                add(s0 + j * w // 8, "z_transpose", k, j)
                add(s0 + j * w // 8 + LAG["affine"], "affine", k, j, j in V_EVAC or (first >= V_TAIL and j % 2 == 1))
            ends = ((w + 1) // 2, w)
            for g in range(2):
                il = s0 + ends[g] - 1 + LAG["affine"] + LAG["interleave"]
                add(il, "interleave", k, g)
                add(il + LAG["h_quant"], "h_quant", k, g)
            for i in range(w):
                step = il + LAG["h_quant"] + LAG["mm2"] + i
                add(step, "mm2", first + i)
                add(step + LAG["gelu"], "gelu", first + i)
                if (first + i) % 2 == 1:
                    add(step + LAG["gelu"], "store_act", (first + i) // 2)
        stages = {
            "dequant": dequant, "a_transpose": a_transpose, "a_evac": a_evac, "a_quant": a_quant, "mm1": mm1,
            "resid": resid, "mean": mean, "square": square, "var": var, "norm": norm, "shift": shift, "normalize": normalize,
            "z_transpose": z_transpose, "affine": affine, "interleave": interleave, "h_quant": h_quant,
            "mm2": mm2, "gelu": gelu, "store_mid": store_mid, "store_act": store_act,
        }
        loaded = 0
        for step, rank, serial, args in sorted(jobs):
            while loaded <= step // MT and loaded < MACROS:
                if loaded + 3 < MACROS:
                    load_a(loaded + 3)
                if loaded + 2 < MACROS:
                    load_x(loaded + 2)
                loaded += 1
            stages[RANK[rank]](*args)
